import numpy as np
import ml_dtypes


def mxq(x, axis, fmt="e4m3"):
    dtype, down = {"e4m3": (ml_dtypes.float8_e4m3fn, 7), "e5m2": (ml_dtypes.float8_e5m2, 14)}[fmt]
    v = np.moveaxis(np.asarray(x, np.float32).astype(ml_dtypes.bfloat16).astype(np.float64), axis, -1)
    blocks = v.reshape(v.shape[:-1] + (-1, 32))
    amax = np.abs(blocks).max(-1, keepdims=True)
    byte = np.maximum(np.where(amax > 0, np.frexp(amax)[1] - 1 + 127, 0) - down, 1)
    scale = np.exp2(byte - 127.0)
    codes = (blocks / scale).astype(np.float32).astype(dtype).astype(np.float64)
    return np.moveaxis((codes * scale).reshape(v.shape), -1, axis)


WIDE = False


def mx_kscale(k):
    if not WIDE:
        return np.ones(k)
    levels = np.array([10, -10, 5, -5, 0])
    a = np.random.permutation(np.resize(levels, k // 512 * 4)).reshape(k // 512, 4)
    idx = np.arange(k)
    return np.exp2(a[idx // 512, idx % 128 // 32])


BF16 = ml_dtypes.bfloat16


def bf(x):
    return np.asarray(x, np.float32).astype(BF16)


def f64(x):
    return np.asarray(x).astype(np.float64)


B, T, D, H = 8, 1024, 512, 2048
R = B * T


def sigmoid(v):
    return 1.0 / (1.0 + np.exp(-v))


def setup_inputs():
    s, t = mx_kscale(D), mx_kscale(D)
    n = np.random.standard_normal
    return {"h": bf(n((B, T, D)) * s), "yt": bf(n((B, T, D)) * 0.5 * t),
            "Wq": bf(n((D, D)) * 1.5 / np.sqrt(D) / s[:, None]), "bq": bf(0.3 * n(D)),
            "Wo": bf(n((D, D)) * 2.5 / np.sqrt(D) / t[:, None]), "bo": bf(0.3 * n(D))}


def reference(h, yt, Wq, bq, Wo, bo):
    q = (mxq(f64(h).reshape(R, D), 1, "e4m3") @ mxq(f64(Wq), 0, "e4m3")) + f64(bq)
    y = sigmoid(q) * f64(yt).reshape(R, D)
    attn = (mxq(y, 1, "e4m3") @ mxq(f64(Wo), 0, "e4m3")) + f64(bo)
    return attn.reshape(B, T, D)

@@ -1,0 +1,251 @@
+from contextlib import ExitStack
+
+import concourse.mybir as mybir
+from concourse.masks import make_identity
+
+F32 = mybir.dt.float32
+BF16 = mybir.dt.bfloat16
+U32 = mybir.dt.uint32
+U8 = mybir.dt.uint8
+FP8X4 = mybir.dt.float8_e4m3fn_x4
+SIGMOID = mybir.ActivationFunctionType.Sigmoid
+ADD = mybir.AluOpType.add
+MULT = mybir.AluOpType.mult
+
+ROWS = 8 * 1024
+D = 512
+P = 128
+PACK = 4
+CHUNK = 512
+CHUNKS = ROWS // CHUNK
+ROW_TILES = CHUNK // P
+HALF = CHUNK // 2
+BANK = 512
+LOOKAHEAD = 3
+
+FLOPS = 2 * 2 * ROWS * D * D
+
+
+def tile_attentionfreetransformerencoder_pb_t_kernel(tc, h, yt, Wq, bq, Wo, bo, out):
+    nc = tc.nc
+
+    h_chunks = h.flatten_outer_dims().rearrange("(c p j) d -> c p (j d)", p=P, j=ROW_TILES)
+    yt_chunks = yt.flatten_outer_dims().rearrange("(c p j) d -> c p (j d)", p=P, j=ROW_TILES)
+    out_chunks = out.flatten_outer_dims().rearrange("(c p j) d -> c p (j d)", p=P, j=ROW_TILES)
+
+    with ExitStack() as ctx:
+        consts = ctx.enter_context(tc.tile_pool(name="consts", bufs=1))
+        h_pool = ctx.enter_context(tc.tile_pool(name="h_pool", bufs=LOOKAHEAD + 1))
+        yt_pool = ctx.enter_context(tc.tile_pool(name="yt_pool", bufs=LOOKAHEAD + 3))
+        work = ctx.enter_context(tc.tile_pool(name="work", bufs=3))
+        out_pool = ctx.enter_context(tc.tile_pool(name="out_pool", bufs=4))
+        psum = ctx.enter_context(tc.psum_pool(name="psum", bufs=2))
+
+        warm = consts.tile([P, 1], F32, name="warm")
+        nc.vector.memset(warm[:], 0.0)
+        nc.scalar.activation(out=warm[:], in_=warm[:], func=SIGMOID)
+
+        ident = consts.tile([P, P], F32, name="ident")
+        make_identity(nc, ident[:])
+
+        def load_weight(w, name):
+            raw = consts.tile([P, PACK * D], BF16, name=name)
+            nc.sync.dma_start(
+                out=raw[:].rearrange("p (u x) -> p u x", u=2),
+                in_=w.rearrange("(u p e) c -> p u (e c)", u=2, e=2),
+            )
+            return raw
+
+        wq_raw = load_weight(Wq, "wq_raw")
+
+        bq_rows = consts.tile([P, 2 * P], BF16, name="bq_rows")
+        nc.vector.memset(bq_rows[:], 0.0)
+        nc.scalar.dma_start(out=bq_rows[0:2, :], in_=bq.rearrange("(u x) -> u x", u=2))
+
+        bo_rows = consts.tile([P, D], BF16, name="bo_rows")
+        nc.vector.memset(bo_rows[:], 0.0)
+        nc.scalar.dma_start(out=bo_rows[0:1, :], in_=bo.rearrange("(o d) -> o d", o=1))
+        ones = consts.tile([P, P], BF16, name="ones")
+        nc.vector.memset(ones[:], 1.0)
+
+        h_rows = {}
+        yt_rows = {}
+
+        def load_rows(c):
+            h_sb = h_pool.tile([P, ROW_TILES * D], BF16, name="h_sb")
+            nc.sync.dma_start(out=h_sb[:], in_=h_chunks[c])
+            h_rows[c] = h_sb
+            yt_sb = yt_pool.tile([P, ROW_TILES * D], BF16, name="yt_sb")
+            nc.sync.dma_start(out=yt_sb[:], in_=yt_chunks[c])
+            yt_rows[c] = yt_sb
+
+        load_rows(0)
+        wo_raw = load_weight(Wo, "wo_raw")
+        for c in range(1, LOOKAHEAD):
+            load_rows(c)
+
+        wq_grouped = consts.tile([P, D * PACK], BF16, name="wq_grouped", align_bytes=64)
+        wq_from = wq_raw[:].rearrange("p (t u q e) -> p u e q t", t=PACK, u=2, e=2)
+        wq_to = wq_grouped[:].rearrange("p (u e q t) -> p u e q t", u=2, e=2, t=PACK)
+        for u in range(2):
+            for e in range(2):
+                nc.vector.tensor_copy(out=wq_to[:, u, e], in_=wq_from[:, u, e])
+        wq_codes = consts.tile([P, D], U32, name="wq_codes", align_bytes=64)
+        wq_scales = consts.tile([P, D], U8, name="wq_scales", align_bytes=64)
+        nc.vector.quantize_mx(out=wq_codes[:].bitcast(FP8X4), scales=wq_scales[:], in_=wq_grouped[:])
+
+        bq_ps = psum.tile([P, BANK], F32, name="bq_ps", tag="hT")
+        nc.tensor.transpose(bq_ps[:, 0:P], bq_rows[:].bitcast(F32), ident[:])
+        bq_cols = consts.tile([P, PACK], F32, name="bq_cols")
+        nc.vector.tensor_copy(out=bq_cols[:], in_=bq_ps[:, 0:2].bitcast(BF16))
+
+        wo_grouped = consts.tile([P, D * PACK], BF16, name="wo_grouped", align_bytes=64)
+        nc.vector.tensor_copy(
+            out=wo_grouped[:].rearrange("p (c t) -> p c t", t=PACK),
+            in_=wo_raw[:].rearrange("p (t c) -> p c t", t=PACK),
+        )
+        wo_codes = consts.tile([P, D], U32, name="wo_codes", align_bytes=64)
+        wo_scales = consts.tile([P, D], U8, name="wo_scales", align_bytes=64)
+        nc.vector.quantize_mx(out=wo_codes[:].bitcast(FP8X4), scales=wo_scales[:], in_=wo_grouped[:])
+
+        bo_ps = psum.tile([P, BANK], F32, name="bo_ps", tag="o")
+        nc.tensor.matmul(out=bo_ps[:], lhsT=ones[:], rhs=bo_rows[:], start=True, stop=True)
+        bo_all = consts.tile([P, D], F32, name="bo_all")
+        nc.vector.tensor_copy(out=bo_all[:], in_=bo_ps[:])
+
+        def transpose_words(bank, rows_sb, half):
+            words = rows_sb[:].bitcast(F32)
+            for j in range(2):
+                first = (2 * half + j) * (D // 2)
+                for u in range(2):
+                    nc.tensor.transpose(
+                        bank[:, u * HALF + j * P : u * HALF + (j + 1) * P],
+                        words[:, first + u * P : first + (u + 1) * P],
+                        ident[:],
+                    )
+
+        h_grouped = {}
+        h_mx = {}
+        yt_banks = {}
+        gates = {}
+        y_grouped = {}
+        y_mx = {}
+        out_rows = {}
+
+        def transpose_h(c, half):
+            if half == 0:
+                grouped = work.tile([P, CHUNK * PACK], BF16, name="h_grouped", align_bytes=64)
+                h_grouped[c] = grouped
+            bank = psum.tile([P, BANK], F32, name="hT", tag="hT")
+            transpose_words(bank, h_rows[c], half)
+            nc.scalar.copy(
+                out=h_grouped[c][:]
+                .bitcast(F32)[:, half * BANK : (half + 1) * BANK]
+                .rearrange("p (r u) -> p r u", u=2),
+                in_=bank[:].rearrange("p (u r) -> p r u", u=2),
+            )
+
+        def quantise_h(c):
+            codes = work.tile([P, CHUNK], U32, name="h_codes", align_bytes=64)
+            scales = work.tile([P, CHUNK], U8, name="h_scales", align_bytes=64)
+            nc.vector.quantize_mx(out=codes[:].bitcast(FP8X4), scales=scales[:], in_=h_grouped[c][:])
+            h_mx[c] = (codes, scales)
+            gate = work.tile([P, PACK * CHUNK], F32, name="gate")
+            gates[c] = gate
+
+        def project_q(c, m):
+            codes, scales = h_mx[c]
+            q_ps = psum.tile([P, BANK], F32, name="q_ps", tag="q")
+            nc.tensor.matmul_mx(
+                out=q_ps[:],
+                lhsT=wq_codes[:, m * P : (m + 1) * P].bitcast(FP8X4),
+                lhsT_scale=wq_scales[:, m * P : (m + 1) * P],
+                rhs=codes[:].bitcast(FP8X4),
+                rhs_scale=scales[:],
+                start=True,
+                stop=True,
+            )
+            nc.scalar.activation(
+                out=gates[c][:, m * CHUNK : (m + 1) * CHUNK],
+                in_=q_ps[:],
+                func=SIGMOID,
+                bias=bq_cols[:, m : m + 1],
+                scale=1.0,
+            )
+
+        def transpose_yt(c, half):
+            bank = psum.tile([P, BANK], F32, name="ytT", tag="ytT")
+            transpose_words(bank, yt_rows[c], half)
+            yt_banks[(c, half)] = bank
+
+        def apply_gate(c, half):
+            if half == 0:
+                grouped = work.tile([P, CHUNK * PACK], BF16, name="y_grouped", align_bytes=64)
+                y_grouped[c] = grouped
+            nc.vector.tensor_tensor(
+                out=y_grouped[c][:, half * HALF * PACK : (half + 1) * HALF * PACK].rearrange(
+                    "p (r u e) -> p r u e", u=2, e=2
+                ),
+                in0=gates[c][:].rearrange("p (u e r) -> p r u e", u=2, e=2)[
+                    :, half * HALF : (half + 1) * HALF
+                ],
+                in1=yt_banks[(c, half)][:].bitcast(BF16).rearrange("p (u r e) -> p r u e", u=2, e=2),
+                op=MULT,
+            )
+
+        def quantise_y(c):
+            codes = work.tile([P, CHUNK], U32, name="y_codes", align_bytes=64)
+            scales = work.tile([P, CHUNK], U8, name="y_scales", align_bytes=64)
+            nc.vector.quantize_mx(out=codes[:].bitcast(FP8X4), scales=scales[:], in_=y_grouped[c][:])
+            y_mx[c] = (codes, scales)
+
+        def project_out(c, j):
+            if j == 0:
+                o_sb = out_pool.tile([P, ROW_TILES * D], F32, name="o_sb")
+                out_rows[c] = o_sb
+            codes, scales = y_mx[c]
+            o_ps = psum.tile([P, BANK], F32, name="o_ps", tag="o")
+            nc.tensor.matmul_mx(
+                out=o_ps[:],
+                lhsT=codes[:, j * P : (j + 1) * P].bitcast(FP8X4),
+                lhsT_scale=scales[:, j * P : (j + 1) * P],
+                rhs=wo_codes[:].bitcast(FP8X4),
+                rhs_scale=wo_scales[:],
+                start=True,
+                stop=True,
+            )
+            dest = out_rows[c][:, j * D : (j + 1) * D]
+            if j % 2 == 0:
+                nc.vector.tensor_tensor(out=dest, in0=o_ps[:], in1=bo_all[:], op=ADD)
+            else:
+                nc.scalar.copy(out=dest, in_=o_ps[:])
+                nc.gpsimd.tensor_tensor(out=dest, in0=dest, in1=bo_all[:], op=ADD)
+
+        def store(c):
+            nc.sync.dma_start(out=out_chunks[c], in_=out_rows[c][:])
+
+        def live(c):
+            return 0 <= c < CHUNKS
+
+        for s in range(CHUNKS + 3):
+            if live(s + LOOKAHEAD):
+                load_rows(s + LOOKAHEAD)
+            for half in range(2):
+                if live(s - 2):
+                    transpose_yt(s - 2, half)
+                if live(s):
+                    transpose_h(s, half)
+            if live(s - 1):
+                quantise_h(s - 1)
+            if live(s - 2):
+                apply_gate(s - 2, 0)
+                apply_gate(s - 2, 1)
+            for k in range(PACK):
+                if live(s - 1):
+                    project_q(s - 1, k)
+                if live(s - 3):
+                    project_out(s - 3, k)
+            if live(s - 2):
+                quantise_y(s - 2)
+            if live(s - 3):
+                store(s - 3)

@@ -23,6 +23,11 @@ HALF = CHUNK // 2
 BANK = 512
 LOOKAHEAD = 3
 
+AT_QUANTISE_H = 1
+AT_PROJECT_Q = 2
+AT_GATE = 3
+AT_PROJECT_OUT = 4
+
 FLOPS = 2 * 2 * ROWS * D * D
 
 
@@ -34,19 +39,35 @@ def tile_attentionfreetransformerencoder_pb_t_kernel(tc, h, yt, Wq, bq, Wo, bo, 
     out_chunks = out.flatten_outer_dims().rearrange("(c p j) d -> c p (j d)", p=P, j=ROW_TILES)
 
     with ExitStack() as ctx:
+        ctx.enter_context(tc.manual_schedule())
+
         consts = ctx.enter_context(tc.tile_pool(name="consts", bufs=1))
-        h_pool = ctx.enter_context(tc.tile_pool(name="h_pool", bufs=LOOKAHEAD + 1))
-        yt_pool = ctx.enter_context(tc.tile_pool(name="yt_pool", bufs=LOOKAHEAD + 3))
+        rows_in = ctx.enter_context(tc.tile_pool(name="rows_in", bufs=LOOKAHEAD + 1))
         work = ctx.enter_context(tc.tile_pool(name="work", bufs=3))
-        out_pool = ctx.enter_context(tc.tile_pool(name="out_pool", bufs=4))
-        psum = ctx.enter_context(tc.psum_pool(name="psum", bufs=2))
+        rows_out = ctx.enter_context(tc.tile_pool(name="rows_out", bufs=4))
+        for_scalar = ctx.enter_context(tc.psum_pool(name="for_scalar", bufs=4))
+        for_vector = ctx.enter_context(tc.psum_pool(name="for_vector", bufs=4))
 
-        warm = consts.tile([P, 1], F32, name="warm")
-        nc.vector.memset(warm[:], 0.0)
-        nc.scalar.activation(out=warm[:], in_=warm[:], func=SIGMOID)
+        def scalar_bank():
+            bank = for_scalar.tile([P, BANK], F32, name="scalar_bank")
+            return bank
 
-        ident = consts.tile([P, P], F32, name="ident")
-        make_identity(nc, ident[:])
+        def vector_bank():
+            bank = for_vector.tile([P, BANK], F32, name="vector_bank")
+            return bank
+
+        h_rows = {}
+        yt_rows = {}
+
+        def load_h(c):
+            h_sb = rows_in.tile([P, ROW_TILES * D], BF16, name="h_sb")
+            nc.sync.dma_start(out=h_sb[:], in_=h_chunks[c])
+            h_rows[c] = h_sb
+
+        def load_yt(c):
+            yt_sb = rows_in.tile([P, ROW_TILES * D], BF16, name="yt_sb")
+            nc.sync.dma_start(out=yt_sb[:], in_=yt_chunks[c])
+            yt_rows[c] = yt_sb
 
         def load_weight(w, name):
             raw = consts.tile([P, PACK * D], BF16, name=name)
@@ -56,33 +77,27 @@ def tile_attentionfreetransformerencoder_pb_t_kernel(tc, h, yt, Wq, bq, Wo, bo, 
             )
             return raw
 
-        wq_raw = load_weight(Wq, "wq_raw")
-
         bq_rows = consts.tile([P, 2 * P], BF16, name="bq_rows")
         nc.vector.memset(bq_rows[:], 0.0)
         nc.scalar.dma_start(out=bq_rows[0:2, :], in_=bq.rearrange("(u x) -> u x", u=2))
-
         bo_rows = consts.tile([P, D], BF16, name="bo_rows")
         nc.vector.memset(bo_rows[:], 0.0)
         nc.scalar.dma_start(out=bo_rows[0:1, :], in_=bo.rearrange("(o d) -> o d", o=1))
         ones = consts.tile([P, P], BF16, name="ones")
         nc.vector.memset(ones[:], 1.0)
 
-        h_rows = {}
-        yt_rows = {}
-
-        def load_rows(c):
-            h_sb = h_pool.tile([P, ROW_TILES * D], BF16, name="h_sb")
-            nc.sync.dma_start(out=h_sb[:], in_=h_chunks[c])
-            h_rows[c] = h_sb
-            yt_sb = yt_pool.tile([P, ROW_TILES * D], BF16, name="yt_sb")
-            nc.sync.dma_start(out=yt_sb[:], in_=yt_chunks[c])
-            yt_rows[c] = yt_sb
-
-        load_rows(0)
-        wo_raw = load_weight(Wo, "wo_raw")
+        load_h(0)
+        wq_raw = load_weight(Wq, "wq_raw")
         for c in range(1, LOOKAHEAD):
-            load_rows(c)
+            load_h(c)
+        wo_raw = load_weight(Wo, "wo_raw")
+
+        warm = consts.tile([P, 1], F32, name="warm")
+        nc.vector.memset(warm[:], 0.0)
+        nc.scalar.activation(out=warm[:], in_=warm[:], func=SIGMOID)
+
+        ident = consts.tile([P, P], F32, name="ident")
+        make_identity(nc, ident[:])
 
         wq_grouped = consts.tile([P, D * PACK], BF16, name="wq_grouped", align_bytes=64)
         wq_from = wq_raw[:].rearrange("p (t u q e) -> p u e q t", t=PACK, u=2, e=2)
@@ -94,24 +109,27 @@ def tile_attentionfreetransformerencoder_pb_t_kernel(tc, h, yt, Wq, bq, Wo, bo, 
         wq_scales = consts.tile([P, D], U8, name="wq_scales", align_bytes=64)
         nc.vector.quantize_mx(out=wq_codes[:].bitcast(FP8X4), scales=wq_scales[:], in_=wq_grouped[:])
 
-        bq_ps = psum.tile([P, BANK], F32, name="bq_ps", tag="hT")
+        bq_ps = vector_bank()
         nc.tensor.transpose(bq_ps[:, 0:P], bq_rows[:].bitcast(F32), ident[:])
         bq_cols = consts.tile([P, PACK], F32, name="bq_cols")
         nc.vector.tensor_copy(out=bq_cols[:], in_=bq_ps[:, 0:2].bitcast(BF16))
 
-        wo_grouped = consts.tile([P, D * PACK], BF16, name="wo_grouped", align_bytes=64)
-        nc.vector.tensor_copy(
-            out=wo_grouped[:].rearrange("p (c t) -> p c t", t=PACK),
-            in_=wo_raw[:].rearrange("p (t c) -> p c t", t=PACK),
-        )
         wo_codes = consts.tile([P, D], U32, name="wo_codes", align_bytes=64)
         wo_scales = consts.tile([P, D], U8, name="wo_scales", align_bytes=64)
-        nc.vector.quantize_mx(out=wo_codes[:].bitcast(FP8X4), scales=wo_scales[:], in_=wo_grouped[:])
-
-        bo_ps = psum.tile([P, BANK], F32, name="bo_ps", tag="o")
-        nc.tensor.matmul(out=bo_ps[:], lhsT=ones[:], rhs=bo_rows[:], start=True, stop=True)
         bo_all = consts.tile([P, D], F32, name="bo_all")
-        nc.vector.tensor_copy(out=bo_all[:], in_=bo_ps[:])
+
+        def prepare_second_product():
+            wo_grouped = consts.tile([P, D * PACK], BF16, name="wo_grouped", align_bytes=64)
+            nc.vector.tensor_copy(
+                out=wo_grouped[:].rearrange("p (c t) -> p c t", t=PACK),
+                in_=wo_raw[:].rearrange("p (t c) -> p c t", t=PACK),
+            )
+            bo_ps = vector_bank()
+            nc.tensor.matmul(out=bo_ps[:], lhsT=ones[:], rhs=bo_rows[:], start=True, stop=True)
+            nc.vector.tensor_copy(out=bo_all[:], in_=bo_ps[:])
+            nc.vector.quantize_mx(
+                out=wo_codes[:].bitcast(FP8X4), scales=wo_scales[:], in_=wo_grouped[:]
+            )
 
         def transpose_words(bank, rows_sb, half):
             words = rows_sb[:].bitcast(F32)
@@ -136,7 +154,7 @@ def tile_attentionfreetransformerencoder_pb_t_kernel(tc, h, yt, Wq, bq, Wo, bo, 
             if half == 0:
                 grouped = work.tile([P, CHUNK * PACK], BF16, name="h_grouped", align_bytes=64)
                 h_grouped[c] = grouped
-            bank = psum.tile([P, BANK], F32, name="hT", tag="hT")
+            bank = scalar_bank()
             transpose_words(bank, h_rows[c], half)
             nc.scalar.copy(
                 out=h_grouped[c][:]
@@ -150,12 +168,13 @@ def tile_attentionfreetransformerencoder_pb_t_kernel(tc, h, yt, Wq, bq, Wo, bo, 
             scales = work.tile([P, CHUNK], U8, name="h_scales", align_bytes=64)
             nc.vector.quantize_mx(out=codes[:].bitcast(FP8X4), scales=scales[:], in_=h_grouped[c][:])
             h_mx[c] = (codes, scales)
-            gate = work.tile([P, PACK * CHUNK], F32, name="gate")
-            gates[c] = gate
 
         def project_q(c, m):
+            if m == 0:
+                gate = work.tile([P, PACK * CHUNK], F32, name="gate")
+                gates[c] = gate
             codes, scales = h_mx[c]
-            q_ps = psum.tile([P, BANK], F32, name="q_ps", tag="q")
+            q_ps = scalar_bank()
             nc.tensor.matmul_mx(
                 out=q_ps[:],
                 lhsT=wq_codes[:, m * P : (m + 1) * P].bitcast(FP8X4),
@@ -174,7 +193,7 @@ def tile_attentionfreetransformerencoder_pb_t_kernel(tc, h, yt, Wq, bq, Wo, bo, 
             )
 
         def transpose_yt(c, half):
-            bank = psum.tile([P, BANK], F32, name="ytT", tag="ytT")
+            bank = vector_bank()
             transpose_words(bank, yt_rows[c], half)
             yt_banks[(c, half)] = bank
 
@@ -201,10 +220,11 @@ def tile_attentionfreetransformerencoder_pb_t_kernel(tc, h, yt, Wq, bq, Wo, bo, 
 
         def project_out(c, j):
             if j == 0:
-                o_sb = out_pool.tile([P, ROW_TILES * D], F32, name="o_sb")
+                o_sb = rows_out.tile([P, ROW_TILES * D], F32, name="o_sb")
                 out_rows[c] = o_sb
             codes, scales = y_mx[c]
-            o_ps = psum.tile([P, BANK], F32, name="o_ps", tag="o")
+            through_vector = j % 2 == 0
+            o_ps = vector_bank() if through_vector else scalar_bank()
             nc.tensor.matmul_mx(
                 out=o_ps[:],
                 lhsT=codes[:, j * P : (j + 1) * P].bitcast(FP8X4),
@@ -215,7 +235,7 @@ def tile_attentionfreetransformerencoder_pb_t_kernel(tc, h, yt, Wq, bq, Wo, bo, 
                 stop=True,
             )
             dest = out_rows[c][:, j * D : (j + 1) * D]
-            if j % 2 == 0:
+            if through_vector:
                 nc.vector.tensor_tensor(out=dest, in0=o_ps[:], in1=bo_all[:], op=ADD)
             else:
                 nc.scalar.copy(out=dest, in_=o_ps[:])
@@ -227,25 +247,28 @@ def tile_attentionfreetransformerencoder_pb_t_kernel(tc, h, yt, Wq, bq, Wo, bo, 
         def live(c):
             return 0 <= c < CHUNKS
 
-        for s in range(CHUNKS + 3):
+        for s in range(CHUNKS + AT_PROJECT_OUT):
             if live(s + LOOKAHEAD):
-                load_rows(s + LOOKAHEAD)
+                load_h(s + LOOKAHEAD)
+            if live(s - AT_GATE + LOOKAHEAD):
+                load_yt(s - AT_GATE + LOOKAHEAD)
+            if s == AT_PROJECT_Q:
+                prepare_second_product()
+            if live(s - AT_QUANTISE_H):
+                quantise_h(s - AT_QUANTISE_H)
             for half in range(2):
-                if live(s - 2):
-                    transpose_yt(s - 2, half)
+                if live(s - AT_GATE):
+                    transpose_yt(s - AT_GATE, half)
                 if live(s):
                     transpose_h(s, half)
-            if live(s - 1):
-                quantise_h(s - 1)
-            if live(s - 2):
-                apply_gate(s - 2, 0)
-                apply_gate(s - 2, 1)
-            for k in range(PACK):
-                if live(s - 1):
-                    project_q(s - 1, k)
-                if live(s - 3):
-                    project_out(s - 3, k)
-            if live(s - 2):
-                quantise_y(s - 2)
-            if live(s - 3):
-                store(s - 3)
+                if live(s - AT_GATE):
+                    apply_gate(s - AT_GATE, half)
+                for k in (2 * half, 2 * half + 1):
+                    if live(s - AT_PROJECT_Q):
+                        project_q(s - AT_PROJECT_Q, k)
+                    if live(s - AT_PROJECT_OUT):
+                        project_out(s - AT_PROJECT_OUT, k)
+            if live(s - AT_GATE):
+                quantise_y(s - AT_GATE)
+            if live(s - AT_PROJECT_OUT):
+                store(s - AT_PROJECT_OUT)

@@ -26,7 +26,8 @@ LOOKAHEAD = 3
 AT_QUANTISE_H = 1
 AT_PROJECT_Q = 2
 AT_GATE = 3
-AT_PROJECT_OUT = 4
+AT_QUANTISE_Y = 4
+AT_PROJECT_OUT = 5
 
 FLOPS = 2 * 2 * ROWS * D * D
 
@@ -86,9 +87,8 @@ def tile_attentionfreetransformerencoder_pb_t_kernel(tc, h, yt, Wq, bq, Wo, bo, 
         ones = consts.tile([P, P], BF16, name="ones")
         nc.vector.memset(ones[:], 1.0)
 
-        load_h(0)
         wq_raw = load_weight(Wq, "wq_raw")
-        for c in range(1, LOOKAHEAD):
+        for c in range(LOOKAHEAD):
             load_h(c)
         wo_raw = load_weight(Wo, "wo_raw")
 
@@ -109,10 +109,12 @@ def tile_attentionfreetransformerencoder_pb_t_kernel(tc, h, yt, Wq, bq, Wo, bo, 
         wq_scales = consts.tile([P, D], U8, name="wq_scales", align_bytes=64)
         nc.vector.quantize_mx(out=wq_codes[:].bitcast(FP8X4), scales=wq_scales[:], in_=wq_grouped[:])
 
-        bq_ps = vector_bank()
-        nc.tensor.transpose(bq_ps[:, 0:P], bq_rows[:].bitcast(F32), ident[:])
         bq_cols = consts.tile([P, PACK], F32, name="bq_cols")
-        nc.vector.tensor_copy(out=bq_cols[:], in_=bq_ps[:, 0:2].bitcast(BF16))
+
+        def stand_bq_up():
+            bq_ps = vector_bank()
+            nc.tensor.transpose(bq_ps[:, 0:P], bq_rows[:].bitcast(F32), ident[:])
+            nc.vector.tensor_copy(out=bq_cols[:], in_=bq_ps[:, 0:2].bitcast(BF16))
 
         wo_codes = consts.tile([P, D], U32, name="wo_codes", align_bytes=64)
         wo_scales = consts.tile([P, D], U8, name="wo_scales", align_bytes=64)
@@ -223,7 +225,7 @@ def tile_attentionfreetransformerencoder_pb_t_kernel(tc, h, yt, Wq, bq, Wo, bo, 
                 o_sb = rows_out.tile([P, ROW_TILES * D], F32, name="o_sb")
                 out_rows[c] = o_sb
             codes, scales = y_mx[c]
-            through_vector = j % 2 == 0
+            through_vector = j % 2 == 0 or c == CHUNKS - 1
             o_ps = vector_bank() if through_vector else scalar_bank()
             nc.tensor.matmul_mx(
                 out=o_ps[:],
@@ -240,9 +242,9 @@ def tile_attentionfreetransformerencoder_pb_t_kernel(tc, h, yt, Wq, bq, Wo, bo, 
             else:
                 nc.scalar.copy(out=dest, in_=o_ps[:])
                 nc.gpsimd.tensor_tensor(out=dest, in0=dest, in1=bo_all[:], op=ADD)
-
-        def store(c):
-            nc.sync.dma_start(out=out_chunks[c], in_=out_rows[c][:])
+            if j % 2 == 1:
+                pair = slice((j - 1) * D, (j + 1) * D)
+                nc.sync.dma_start(out=out_chunks[c][:, pair], in_=out_rows[c][:, pair])
 
         def live(c):
             return 0 <= c < CHUNKS
@@ -252,23 +254,22 @@ def tile_attentionfreetransformerencoder_pb_t_kernel(tc, h, yt, Wq, bq, Wo, bo, 
                 load_h(s + LOOKAHEAD)
             if live(s - AT_GATE + LOOKAHEAD):
                 load_yt(s - AT_GATE + LOOKAHEAD)
-            if s == AT_PROJECT_Q:
-                prepare_second_product()
+            if live(s - AT_QUANTISE_Y):
+                quantise_y(s - AT_QUANTISE_Y)
             if live(s - AT_QUANTISE_H):
                 quantise_h(s - AT_QUANTISE_H)
+            if s == AT_PROJECT_Q - 1:
+                stand_bq_up()
+            if s == AT_PROJECT_Q:
+                prepare_second_product()
             for half in range(2):
                 if live(s - AT_GATE):
                     transpose_yt(s - AT_GATE, half)
+                    apply_gate(s - AT_GATE, half)
                 if live(s):
                     transpose_h(s, half)
-                if live(s - AT_GATE):
-                    apply_gate(s - AT_GATE, half)
                 for k in (2 * half, 2 * half + 1):
                     if live(s - AT_PROJECT_Q):
                         project_q(s - AT_PROJECT_Q, k)
                     if live(s - AT_PROJECT_OUT):
                         project_out(s - AT_PROJECT_OUT, k)
-            if live(s - AT_GATE):
-                quantise_y(s - AT_GATE)
-            if live(s - AT_PROJECT_OUT):
-                store(s - AT_PROJECT_OUT)

@@ -225,7 +225,7 @@ def tile_attentionfreetransformerencoder_pb_t_kernel(tc, h, yt, Wq, bq, Wo, bo, 
                 o_sb = rows_out.tile([P, ROW_TILES * D], F32, name="o_sb")
                 out_rows[c] = o_sb
             codes, scales = y_mx[c]
-            through_vector = j % 2 == 0 or c == CHUNKS - 1
+            through_vector = j == 0 or (j == 2 and c % 2 == 0) or c == CHUNKS - 1
             o_ps = vector_bank() if through_vector else scalar_bank()
             nc.tensor.matmul_mx(
                 out=o_ps[:],

@@ -23,10 +23,8 @@ HALF = CHUNK // 2
 BANK = 512
 LOOKAHEAD = 3
 
-AT_QUANTISE_H = 1
 AT_PROJECT_Q = 2
 AT_GATE = 3
-AT_QUANTISE_Y = 4
 AT_PROJECT_OUT = 5
 
 FLOPS = 2 * 2 * ROWS * D * D
@@ -144,45 +142,56 @@ def tile_attentionfreetransformerencoder_pb_t_kernel(tc, h, yt, Wq, bq, Wo, bo, 
                         ident[:],
                     )
 
-        h_grouped = {}
-        h_mx = {}
+        grouped = {}
+        mx = {}
+        Y_PART = 0
+        H_PART = 1
         yt_banks = {}
         gates = {}
-        y_grouped = {}
-        y_mx = {}
         out_rows = {}
 
+        def live(c):
+            return 0 <= c < CHUNKS
+
+        def open_step(s):
+            values = work.tile([P, 2 * CHUNK * PACK], BF16, name="grouped", align_bytes=64)
+            grouped[s] = values
+
+        def quantise(s):
+            first = Y_PART if live(s - AT_GATE) else H_PART
+            last = H_PART if live(s) else Y_PART
+            codes = work.tile([P, 2 * CHUNK], U32, name="codes", align_bytes=64)
+            scales = work.tile([P, 2 * CHUNK], U8, name="scales", align_bytes=64)
+            nc.vector.quantize_mx(
+                out=codes[:, first * CHUNK : (last + 1) * CHUNK].bitcast(FP8X4),
+                scales=scales[:, first * CHUNK : (last + 1) * CHUNK],
+                in_=grouped[s][:, first * CHUNK * PACK : (last + 1) * CHUNK * PACK],
+            )
+            mx[s] = (codes, scales)
+
         def transpose_h(c, half):
-            if half == 0:
-                grouped = work.tile([P, CHUNK * PACK], BF16, name="h_grouped", align_bytes=64)
-                h_grouped[c] = grouped
             bank = scalar_bank()
             transpose_words(bank, h_rows[c], half)
+            first_word = (2 * H_PART + half) * BANK
             nc.scalar.copy(
-                out=h_grouped[c][:]
-                .bitcast(F32)[:, half * BANK : (half + 1) * BANK]
+                out=grouped[c][:]
+                .bitcast(F32)[:, first_word : first_word + BANK]
                 .rearrange("p (r u) -> p r u", u=2),
                 in_=bank[:].rearrange("p (u r) -> p r u", u=2),
             )
-
-        def quantise_h(c):
-            codes = work.tile([P, CHUNK], U32, name="h_codes", align_bytes=64)
-            scales = work.tile([P, CHUNK], U8, name="h_scales", align_bytes=64)
-            nc.vector.quantize_mx(out=codes[:].bitcast(FP8X4), scales=scales[:], in_=h_grouped[c][:])
-            h_mx[c] = (codes, scales)
 
         def project_q(c, m):
             if m == 0:
                 gate = work.tile([P, PACK * CHUNK], F32, name="gate")
                 gates[c] = gate
-            codes, scales = h_mx[c]
+            codes, scales = mx[c]
             q_ps = scalar_bank()
             nc.tensor.matmul_mx(
                 out=q_ps[:],
                 lhsT=wq_codes[:, m * P : (m + 1) * P].bitcast(FP8X4),
                 lhsT_scale=wq_scales[:, m * P : (m + 1) * P],
-                rhs=codes[:].bitcast(FP8X4),
-                rhs_scale=scales[:],
+                rhs=codes[:, H_PART * CHUNK : (H_PART + 1) * CHUNK].bitcast(FP8X4),
+                rhs_scale=scales[:, H_PART * CHUNK : (H_PART + 1) * CHUNK],
                 start=True,
                 stop=True,
             )
@@ -200,11 +209,9 @@ def tile_attentionfreetransformerencoder_pb_t_kernel(tc, h, yt, Wq, bq, Wo, bo, 
             yt_banks[(c, half)] = bank
 
         def apply_gate(c, half):
-            if half == 0:
-                grouped = work.tile([P, CHUNK * PACK], BF16, name="y_grouped", align_bytes=64)
-                y_grouped[c] = grouped
+            first_value = (2 * Y_PART + half) * HALF * PACK
             nc.vector.tensor_tensor(
-                out=y_grouped[c][:, half * HALF * PACK : (half + 1) * HALF * PACK].rearrange(
+                out=grouped[c + AT_GATE][:, first_value : first_value + HALF * PACK].rearrange(
                     "p (r u e) -> p r u e", u=2, e=2
                 ),
                 in0=gates[c][:].rearrange("p (u e r) -> p r u e", u=2, e=2)[
@@ -214,23 +221,18 @@ def tile_attentionfreetransformerencoder_pb_t_kernel(tc, h, yt, Wq, bq, Wo, bo, 
                 op=MULT,
             )
 
-        def quantise_y(c):
-            codes = work.tile([P, CHUNK], U32, name="y_codes", align_bytes=64)
-            scales = work.tile([P, CHUNK], U8, name="y_scales", align_bytes=64)
-            nc.vector.quantize_mx(out=codes[:].bitcast(FP8X4), scales=scales[:], in_=y_grouped[c][:])
-            y_mx[c] = (codes, scales)
-
         def project_out(c, j):
             if j == 0:
                 o_sb = rows_out.tile([P, ROW_TILES * D], F32, name="o_sb")
                 out_rows[c] = o_sb
-            codes, scales = y_mx[c]
-            through_vector = j == 0 or (j == 2 and c % 2 == 0) or c == CHUNKS - 1
+            codes, scales = mx[c + AT_GATE]
+            first_row = Y_PART * CHUNK + j * P
+            through_vector = j % 2 == 0 or c == CHUNKS - 1
             o_ps = vector_bank() if through_vector else scalar_bank()
             nc.tensor.matmul_mx(
                 out=o_ps[:],
-                lhsT=codes[:, j * P : (j + 1) * P].bitcast(FP8X4),
-                lhsT_scale=scales[:, j * P : (j + 1) * P],
+                lhsT=codes[:, first_row : first_row + P].bitcast(FP8X4),
+                lhsT_scale=scales[:, first_row : first_row + P],
                 rhs=wo_codes[:].bitcast(FP8X4),
                 rhs_scale=wo_scales[:],
                 start=True,
@@ -246,18 +248,15 @@ def tile_attentionfreetransformerencoder_pb_t_kernel(tc, h, yt, Wq, bq, Wo, bo, 
                 pair = slice((j - 1) * D, (j + 1) * D)
                 nc.sync.dma_start(out=out_chunks[c][:, pair], in_=out_rows[c][:, pair])
 
-        def live(c):
-            return 0 <= c < CHUNKS
-
         for s in range(CHUNKS + AT_PROJECT_OUT):
             if live(s + LOOKAHEAD):
                 load_h(s + LOOKAHEAD)
             if live(s - AT_GATE + LOOKAHEAD):
                 load_yt(s - AT_GATE + LOOKAHEAD)
-            if live(s - AT_QUANTISE_Y):
-                quantise_y(s - AT_QUANTISE_Y)
-            if live(s - AT_QUANTISE_H):
-                quantise_h(s - AT_QUANTISE_H)
+            if live(s - 1) or live(s - 1 - AT_GATE):
+                quantise(s - 1)
+            if live(s) or live(s - AT_GATE):
+                open_step(s)
             if s == AT_PROJECT_Q - 1:
                 stand_bq_up()
             if s == AT_PROJECT_Q:

from contextlib import ExitStack

import concourse.mybir as mybir
from concourse.masks import make_identity

F32 = mybir.dt.float32
BF16 = mybir.dt.bfloat16
U32 = mybir.dt.uint32
U8 = mybir.dt.uint8
FP8X4 = mybir.dt.float8_e4m3fn_x4
SIGMOID = mybir.ActivationFunctionType.Sigmoid
ADD = mybir.AluOpType.add
MULT = mybir.AluOpType.mult

ROWS = 8 * 1024
D = 512
P = 128
PACK = 4
CHUNK = 512
CHUNKS = ROWS // CHUNK
ROW_TILES = CHUNK // P
HALF = CHUNK // 2
BANK = 512
LOOKAHEAD = 3

AT_PROJECT_Q = 2
AT_GATE = 3
AT_PROJECT_OUT = 5

FLOPS = 2 * 2 * ROWS * D * D


def tile_attentionfreetransformerencoder_pb_t_kernel(tc, h, yt, Wq, bq, Wo, bo, out):
    nc = tc.nc

    h_chunks = h.flatten_outer_dims().rearrange("(c p j) d -> c p (j d)", p=P, j=ROW_TILES)
    yt_chunks = yt.flatten_outer_dims().rearrange("(c p j) d -> c p (j d)", p=P, j=ROW_TILES)
    out_chunks = out.flatten_outer_dims().rearrange("(c p j) d -> c p (j d)", p=P, j=ROW_TILES)

    with ExitStack() as ctx:
        ctx.enter_context(tc.manual_schedule())

        consts = ctx.enter_context(tc.tile_pool(name="consts", bufs=1))
        rows_in = ctx.enter_context(tc.tile_pool(name="rows_in", bufs=LOOKAHEAD + 1))
        work = ctx.enter_context(tc.tile_pool(name="work", bufs=3))
        rows_out = ctx.enter_context(tc.tile_pool(name="rows_out", bufs=4))
        for_scalar = ctx.enter_context(tc.psum_pool(name="for_scalar", bufs=4))
        for_vector = ctx.enter_context(tc.psum_pool(name="for_vector", bufs=4))

        def scalar_bank():
            bank = for_scalar.tile([P, BANK], F32, name="scalar_bank")
            return bank

        def vector_bank():
            bank = for_vector.tile([P, BANK], F32, name="vector_bank")
            return bank

        h_rows = {}
        yt_rows = {}

        def load_h(c):
            h_sb = rows_in.tile([P, ROW_TILES * D], BF16, name="h_sb")
            nc.sync.dma_start(out=h_sb[:], in_=h_chunks[c])
            h_rows[c] = h_sb

        def load_yt(c):
            yt_sb = rows_in.tile([P, ROW_TILES * D], BF16, name="yt_sb")
            nc.sync.dma_start(out=yt_sb[:], in_=yt_chunks[c])
            yt_rows[c] = yt_sb

        def load_weight(w, name):
            raw = consts.tile([P, PACK * D], BF16, name=name)
            nc.sync.dma_start(
                out=raw[:].rearrange("p (u x) -> p u x", u=2),
                in_=w.rearrange("(u p e) c -> p u (e c)", u=2, e=2),
            )
            return raw

        bq_rows = consts.tile([P, 2 * P], BF16, name="bq_rows")
        nc.vector.memset(bq_rows[:], 0.0)
        nc.scalar.dma_start(out=bq_rows[0:2, :], in_=bq.rearrange("(u x) -> u x", u=2))
        bo_rows = consts.tile([P, D], BF16, name="bo_rows")
        nc.vector.memset(bo_rows[:], 0.0)
        nc.scalar.dma_start(out=bo_rows[0:1, :], in_=bo.rearrange("(o d) -> o d", o=1))
        ones = consts.tile([P, P], BF16, name="ones")
        nc.vector.memset(ones[:], 1.0)

        wq_raw = load_weight(Wq, "wq_raw")
        for c in range(LOOKAHEAD):
            load_h(c)
        wo_raw = load_weight(Wo, "wo_raw")

        warm = consts.tile([P, 1], F32, name="warm")
        nc.vector.memset(warm[:], 0.0)
        nc.scalar.activation(out=warm[:], in_=warm[:], func=SIGMOID)

        ident = consts.tile([P, P], F32, name="ident")
        make_identity(nc, ident[:])

        wq_grouped = consts.tile([P, D * PACK], BF16, name="wq_grouped", align_bytes=64)
        wq_from = wq_raw[:].rearrange("p (t u q e) -> p u e q t", t=PACK, u=2, e=2)
        wq_to = wq_grouped[:].rearrange("p (u e q t) -> p u e q t", u=2, e=2, t=PACK)
        for u in range(2):
            for e in range(2):
                nc.vector.tensor_copy(out=wq_to[:, u, e], in_=wq_from[:, u, e])
        wq_codes = consts.tile([P, D], U32, name="wq_codes", align_bytes=64)
        wq_scales = consts.tile([P, D], U8, name="wq_scales", align_bytes=64)
        nc.vector.quantize_mx(out=wq_codes[:].bitcast(FP8X4), scales=wq_scales[:], in_=wq_grouped[:])

        bq_cols = consts.tile([P, PACK], F32, name="bq_cols")

        def stand_bq_up():
            bq_ps = vector_bank()
            nc.tensor.transpose(bq_ps[:, 0:P], bq_rows[:].bitcast(F32), ident[:])
            nc.vector.tensor_copy(out=bq_cols[:], in_=bq_ps[:, 0:2].bitcast(BF16))

        wo_codes = consts.tile([P, D], U32, name="wo_codes", align_bytes=64)
        wo_scales = consts.tile([P, D], U8, name="wo_scales", align_bytes=64)
        bo_all = consts.tile([P, D], F32, name="bo_all")

        def prepare_second_product():
            wo_grouped = consts.tile([P, D * PACK], BF16, name="wo_grouped", align_bytes=64)
            nc.vector.tensor_copy(
                out=wo_grouped[:].rearrange("p (c t) -> p c t", t=PACK),
                in_=wo_raw[:].rearrange("p (t c) -> p c t", t=PACK),
            )
            bo_ps = vector_bank()
            nc.tensor.matmul(out=bo_ps[:], lhsT=ones[:], rhs=bo_rows[:], start=True, stop=True)
            nc.vector.tensor_copy(out=bo_all[:], in_=bo_ps[:])
            nc.vector.quantize_mx(
                out=wo_codes[:].bitcast(FP8X4), scales=wo_scales[:], in_=wo_grouped[:]
            )

        def transpose_words(bank, rows_sb, half):
            words = rows_sb[:].bitcast(F32)
            for j in range(2):
                first = (2 * half + j) * (D // 2)
                for u in range(2):
                    nc.tensor.transpose(
                        bank[:, u * HALF + j * P : u * HALF + (j + 1) * P],
                        words[:, first + u * P : first + (u + 1) * P],
                        ident[:],
                    )

        grouped = {}
        mx = {}
        Y_PART = 0
        H_PART = 1
        yt_banks = {}
        gates = {}
        out_rows = {}

        def live(c):
            return 0 <= c < CHUNKS

        def open_step(s):
            values = work.tile([P, 2 * CHUNK * PACK], BF16, name="grouped", align_bytes=64)
            grouped[s] = values

        def quantise(s):
            first = Y_PART if live(s - AT_GATE) else H_PART
            last = H_PART if live(s) else Y_PART
            codes = work.tile([P, 2 * CHUNK], U32, name="codes", align_bytes=64)
            scales = work.tile([P, 2 * CHUNK], U8, name="scales", align_bytes=64)
            nc.vector.quantize_mx(
                out=codes[:, first * CHUNK : (last + 1) * CHUNK].bitcast(FP8X4),
                scales=scales[:, first * CHUNK : (last + 1) * CHUNK],
                in_=grouped[s][:, first * CHUNK * PACK : (last + 1) * CHUNK * PACK],
            )
            mx[s] = (codes, scales)

        def transpose_h(c, half):
            bank = scalar_bank()
            transpose_words(bank, h_rows[c], half)
            first_word = (2 * H_PART + half) * BANK
            nc.scalar.copy(
                out=grouped[c][:]
                .bitcast(F32)[:, first_word : first_word + BANK]
                .rearrange("p (r u) -> p r u", u=2),
                in_=bank[:].rearrange("p (u r) -> p r u", u=2),
            )

        def project_q(c, m):
            if m == 0:
                gate = work.tile([P, PACK * CHUNK], F32, name="gate")
                gates[c] = gate
            codes, scales = mx[c]
            q_ps = scalar_bank()
            nc.tensor.matmul_mx(
                out=q_ps[:],
                lhsT=wq_codes[:, m * P : (m + 1) * P].bitcast(FP8X4),
                lhsT_scale=wq_scales[:, m * P : (m + 1) * P],
                rhs=codes[:, H_PART * CHUNK : (H_PART + 1) * CHUNK].bitcast(FP8X4),
                rhs_scale=scales[:, H_PART * CHUNK : (H_PART + 1) * CHUNK],
                start=True,
                stop=True,
            )
            nc.scalar.activation(
                out=gates[c][:, m * CHUNK : (m + 1) * CHUNK],
                in_=q_ps[:],
                func=SIGMOID,
                bias=bq_cols[:, m : m + 1],
                scale=1.0,
            )

        def transpose_yt(c, half):
            bank = vector_bank()
            transpose_words(bank, yt_rows[c], half)
            yt_banks[(c, half)] = bank

        def apply_gate(c, half):
            first_value = (2 * Y_PART + half) * HALF * PACK
            nc.vector.tensor_tensor(
                out=grouped[c + AT_GATE][:, first_value : first_value + HALF * PACK].rearrange(
                    "p (r u e) -> p r u e", u=2, e=2
                ),
                in0=gates[c][:].rearrange("p (u e r) -> p r u e", u=2, e=2)[
                    :, half * HALF : (half + 1) * HALF
                ],
                in1=yt_banks[(c, half)][:].bitcast(BF16).rearrange("p (u r e) -> p r u e", u=2, e=2),
                op=MULT,
            )

        def project_out(c, j):
            if j == 0:
                o_sb = rows_out.tile([P, ROW_TILES * D], F32, name="o_sb")
                out_rows[c] = o_sb
            codes, scales = mx[c + AT_GATE]
            first_row = Y_PART * CHUNK + j * P
            through_vector = j % 2 == 0 or c == CHUNKS - 1
            o_ps = vector_bank() if through_vector else scalar_bank()
            nc.tensor.matmul_mx(
                out=o_ps[:],
                lhsT=codes[:, first_row : first_row + P].bitcast(FP8X4),
                lhsT_scale=scales[:, first_row : first_row + P],
                rhs=wo_codes[:].bitcast(FP8X4),
                rhs_scale=wo_scales[:],
                start=True,
                stop=True,
            )
            dest = out_rows[c][:, j * D : (j + 1) * D]
            if through_vector:
                nc.vector.tensor_tensor(out=dest, in0=o_ps[:], in1=bo_all[:], op=ADD)
            else:
                nc.scalar.copy(out=dest, in_=o_ps[:])
                nc.gpsimd.tensor_tensor(out=dest, in0=dest, in1=bo_all[:], op=ADD)
            if j % 2 == 1:
                pair = slice((j - 1) * D, (j + 1) * D)
                nc.sync.dma_start(out=out_chunks[c][:, pair], in_=out_rows[c][:, pair])

        for s in range(CHUNKS + AT_PROJECT_OUT):
            if live(s + LOOKAHEAD):
                load_h(s + LOOKAHEAD)
            if live(s - AT_GATE + LOOKAHEAD):
                load_yt(s - AT_GATE + LOOKAHEAD)
            if live(s - 1) or live(s - 1 - AT_GATE):
                quantise(s - 1)
            if live(s) or live(s - AT_GATE):
                open_step(s)
            if s == AT_PROJECT_Q - 1:
                stand_bq_up()
            if s == AT_PROJECT_Q:
                prepare_second_product()
            for half in range(2):
                if live(s - AT_GATE):
                    transpose_yt(s - AT_GATE, half)
                    apply_gate(s - AT_GATE, half)
                if live(s):
                    transpose_h(s, half)
                for k in (2 * half, 2 * half + 1):
                    if live(s - AT_PROJECT_Q):
                        project_q(s - AT_PROJECT_Q, k)
                    if live(s - AT_PROJECT_OUT):
                        project_out(s - AT_PROJECT_OUT, k)
